import numpy as np
import ml_dtypes


def mxq(x, axis, fmt="e4m3"):
    dtype, down = {"e4m3": (ml_dtypes.float8_e4m3fn, 7), "e5m2": (ml_dtypes.float8_e5m2, 14)}[fmt]
    v = np.moveaxis(np.asarray(x, np.float32).astype(ml_dtypes.bfloat16).astype(np.float64), axis, -1)
    blocks = v.reshape(v.shape[:-1] + (-1, 32))
    amax = np.abs(blocks).max(-1, keepdims=True)
    byte = np.maximum(np.where(amax > 0, np.frexp(amax)[1] - 1 + 127, 0) - down, 1)
    scale = np.exp2(byte - 127.0)
    codes = (blocks / scale).astype(np.float32).astype(dtype).astype(np.float64)
    return np.moveaxis((codes * scale).reshape(v.shape), -1, axis)


WIDE = False


def mx_kscale(k):
    if not WIDE:
        return np.ones(k)
    levels = np.array([10, -10, 5, -5, 0])
    a = np.random.permutation(np.resize(levels, k // 512 * 4)).reshape(k // 512, 4)
    idx = np.arange(k)
    return np.exp2(a[idx // 512, idx % 128 // 32])


BF16 = ml_dtypes.bfloat16


def bf(x):
    return np.asarray(x, np.float32).astype(BF16)


def f64(x):
    return np.asarray(x).astype(np.float64)


B, N, DIM, H, KD, D = 4, 256, 1024, 12, 64, 128
HD = 2 * KD + D
HQKV = H * HD
EPS = 1e-5


def setup_inputs():
    s = mx_kscale(DIM)
    c = 2.0 ** (-8.0 * np.random.random(HQKV))
    x = np.random.standard_normal((B, N, DIM)) + 0.5 * np.random.standard_normal(DIM)
    return {"x": bf(x * s),
            "qkv_w": bf(np.random.standard_normal((HQKV, DIM)) * c[:, None] / np.sqrt(DIM) / s),
            "qkv_g": bf(2.0 + 0.2 * np.random.standard_normal(HQKV)),
            "qkv_b": bf(0.3 * np.random.standard_normal(HQKV))}


def bn(y, g, b):
    m = y.mean(axis=(0, 1))
    v = ((y - m) ** 2).mean(axis=(0, 1))
    return (y - m) * (g / np.sqrt(v + EPS)) + b


def reference(x, qkv_w, qkv_g, qkv_b):
    y = mxq(f64(x), 2, "e4m3") @ mxq(f64(qkv_w), 1, "e4m3").T
    qkv = bn(y, f64(qkv_g), f64(qkv_b)).reshape(B, N, H, HD)
    q = qkv[..., :KD].transpose(0, 2, 1, 3)
    k = qkv[..., KD:2 * KD].transpose(0, 2, 1, 3)
    v = qkv[..., 2 * KD:].transpose(0, 2, 1, 3)
    return q, k, v

@@ -1,0 +1,223 @@
+from contextlib import ExitStack
+
+import concourse.mybir as mybir
+from concourse.masks import make_identity
+
+F32 = mybir.dt.float32
+BF16 = mybir.dt.bfloat16
+U32 = mybir.dt.uint32
+U8 = mybir.dt.uint8
+FP8X4 = mybir.dt.float8_e4m3fn_x4
+ACT = mybir.ActivationFunctionType
+
+P = 128
+BATCH, TOKENS, DIM = 4, 256, 1024
+HEADS, KD = 12, 64
+EPS = 1e-5
+
+ROWS = BATCH * TOKENS
+ROW_TILES = ROWS // P
+HALF_TILES = ROW_TILES // 2
+HALF_ROWS = HALF_TILES * P
+PASSES = DIM // 512
+WORDS = DIM // 2
+CHUNKS = WORDS // P
+HEAD_TILES = 2
+TILE_CODES = PASSES * P
+
+FLOPS = 2 * ROWS * DIM * HEADS * HEAD_TILES * P
+
+
+def tile_attention_pa_kernel(tc, x, qkv_w, qkv_g, qkv_b, out_q, out_k, out_v):
+    nc = tc.nc
+    with ExitStack() as ctx:
+        keep = ctx.enter_context(tc.tile_pool(name="keep", bufs=1))
+        stage = ctx.enter_context(tc.tile_pool(name="stage", bufs=2))
+        small = ctx.enter_context(tc.tile_pool(name="small", bufs=3))
+        normed = ctx.enter_context(tc.tile_pool(name="normed", bufs=2 * HEAD_TILES))
+        result = ctx.enter_context(tc.tile_pool(name="result", bufs=2 * HEAD_TILES))
+        y_banks = ctx.enter_context(tc.psum_pool(name="y_banks", bufs=4))
+        t_banks = ctx.enter_context(tc.psum_pool(name="t_banks", bufs=4))
+
+        x_rows = x.rearrange("b (tp j) k -> tp b (j k)", j=ROW_TILES)
+        q_rows = out_q.rearrange("b h (tp j) f -> h tp b (j f)", j=ROW_TILES)
+        k_rows = out_k.rearrange("b h (tp j) f -> h tp b (j f)", j=ROW_TILES)
+        v_rows = out_v.rearrange("b h (tp j) f -> h tp b (j f)", j=ROW_TILES)
+        w_rows = qkv_w.rearrange("(ft m) k -> m ft k", m=P)
+
+        x_raw = []
+        w_raw = []
+        for half in range(2):
+            x_raw.append(keep.tile([P, HALF_TILES * DIM], BF16, name="x_raw%d" % half))
+        for h in range(HEADS):
+            w_raw.append(keep.tile([P, HEAD_TILES * DIM], BF16, name="w_raw%d" % h))
+
+        def load_x(half):
+            cols = slice(half * HALF_TILES * DIM, (half + 1) * HALF_TILES * DIM)
+            nc.sync.dma_start(out=x_raw[half][:], in_=x_rows[:, :, cols])
+
+        def load_w(h):
+            nc.sync.dma_start(
+                out=w_raw[h][:].rearrange("p (t k) -> p t k", t=HEAD_TILES),
+                in_=w_rows[:, HEAD_TILES * h : HEAD_TILES * (h + 1), :],
+            )
+
+        load_x(0)
+        load_w(0)
+        load_x(1)
+        for h in range(1, HEADS):
+            load_w(h)
+
+        ident = keep.tile([P, P], F32, name="ident")
+        make_identity(nc, ident[:])
+        one = keep.tile([P, 1], F32, name="one")
+        nc.vector.memset(one[:], 1.0)
+        table_warm = keep.tile([P, 1], F32, name="table_warm")
+        nc.scalar.activation(out=table_warm[:], in_=one[:], func=ACT.Sqrt)
+
+        n_tiles = HEADS * HEAD_TILES
+        gb_rows = keep.tile([P, P], BF16, name="gb_rows")
+        nc.vector.memset(gb_rows[:], 0.0)
+        nc.scalar.dma_start(out=gb_rows[0:n_tiles, :], in_=qkv_g.rearrange("(ft m) -> ft m", m=P))
+        nc.scalar.dma_start(
+            out=gb_rows[32 : 32 + n_tiles, :], in_=qkv_b.rearrange("(ft m) -> ft m", m=P)
+        )
+        gb_rows_f32 = keep.tile([P, P], F32, name="gb_rows_f32")
+        nc.vector.tensor_copy(out=gb_rows_f32[:], in_=gb_rows[:])
+        gb_bank = t_banks.tile([P, CHUNKS, P], F32, tag="t", name="gb_bank")
+        nc.tensor.transpose(gb_bank[:, 0, :], gb_rows_f32[:], ident[:])
+        gain_shift = keep.tile([P, 64], F32, name="gain_shift")
+        nc.vector.tensor_copy(out=gain_shift[:], in_=gb_bank[:, 0, 0:64])
+
+        x_codes = keep.tile([P, 2 * PASSES * HALF_ROWS], U32, name="x_codes", align_bytes=64)
+        x_scales = keep.tile([P, 2 * PASSES * HALF_ROWS], U8, name="x_scales", align_bytes=64)
+        w_codes = keep.tile([P, n_tiles * TILE_CODES], U32, name="w_codes", align_bytes=64)
+        w_scales = keep.tile([P, n_tiles * TILE_CODES], U8, name="w_scales", align_bytes=64)
+
+        def transpose_row_tile(words):
+            bank = t_banks.tile([P, CHUNKS, P], F32, tag="t", name="kt_bank")
+            for c in range(CHUNKS):
+                nc.tensor.transpose(bank[:, c, :], words[:, c * P : (c + 1) * P], ident[:])
+            return bank[:].rearrange("p (g u) r -> p g r u", u=2)
+
+        def quantise_x(half):
+            grouped = stage.tile([P, 4 * PASSES * HALF_ROWS], BF16, name="x_grouped", align_bytes=64)
+            grouped_words = grouped[:].bitcast(F32).rearrange(
+                "p (g j r u) -> p g j r u", g=PASSES, j=HALF_TILES, r=P, u=2
+            )
+            words = x_raw[half][:].bitcast(F32)
+            for j in range(HALF_TILES):
+                pairs = transpose_row_tile(words[:, j * WORDS : (j + 1) * WORDS])
+                if j % 2 == 0:
+                    nc.vector.tensor_copy(out=grouped_words[:, :, j], in_=pairs)
+                else:
+                    nc.scalar.copy(out=grouped_words[:, :, j], in_=pairs)
+            cols = slice(half * PASSES * HALF_ROWS, (half + 1) * PASSES * HALF_ROWS)
+            nc.vector.quantize_mx(
+                out=x_codes[:, cols].bitcast(FP8X4), scales=x_scales[:, cols], in_=grouped[:]
+            )
+
+        def quantise_w(h):
+            grouped = stage.tile([P, 4 * HEAD_TILES * TILE_CODES], BF16, name="w_grouped", align_bytes=64)
+            grouped_words = grouped[:].bitcast(F32).rearrange(
+                "p (t g m u) -> p t g m u", t=HEAD_TILES, g=PASSES, m=P, u=2
+            )
+            words = w_raw[h][:].bitcast(F32)
+            for t in range(HEAD_TILES):
+                pairs = transpose_row_tile(words[:, t * WORDS : (t + 1) * WORDS])
+                nc.vector.tensor_copy(out=grouped_words[:, t], in_=pairs)
+            cols = slice(h * HEAD_TILES * TILE_CODES, (h + 1) * HEAD_TILES * TILE_CODES)
+            nc.vector.quantize_mx(
+                out=w_codes[:, cols].bitcast(FP8X4), scales=w_scales[:, cols], in_=grouped[:]
+            )
+
+        def project_and_normalise(h):
+            stats = small.tile([P, HEAD_TILES, 2, 6], F32, name="stats")
+            mean_var = small.tile([P, HEAD_TILES, 2], F32, name="mean_var")
+            y = []
+            for t in range(HEAD_TILES):
+                for half in range(2):
+                    bank = y_banks.tile([P, HALF_ROWS], F32, tag="y", name="y_bank")
+                    for g in range(PASSES):
+                        w_cols = slice(
+                            ((h * HEAD_TILES + t) * PASSES + g) * P,
+                            ((h * HEAD_TILES + t) * PASSES + g + 1) * P,
+                        )
+                        x_cols = slice(
+                            (half * PASSES + g) * HALF_ROWS, (half * PASSES + g + 1) * HALF_ROWS
+                        )
+                        nc.tensor.matmul_mx(
+                            out=bank[:],
+                            lhsT=w_codes[:, w_cols].bitcast(FP8X4),
+                            lhsT_scale=w_scales[:, w_cols],
+                            rhs=x_codes[:, x_cols].bitcast(FP8X4),
+                            rhs_scale=x_scales[:, x_cols],
+                            start=(g == 0),
+                            stop=(g == PASSES - 1),
+                        )
+                    nc.vector.bn_stats(out=stats[:, t, half, :], in_=bank[:])
+                    y.append(bank)
+                nc.vector.bn_aggr(
+                    out=mean_var[:, t, :], in_=stats[:, t].rearrange("p a s -> p (a s)")
+                )
+            tiles = slice(h * HEAD_TILES, (h + 1) * HEAD_TILES)
+            shifts = slice(32 + h * HEAD_TILES, 32 + (h + 1) * HEAD_TILES)
+            std = small.tile([P, HEAD_TILES], F32, name="std")
+            nc.scalar.activation(out=std[:], in_=mean_var[:, :, 1], func=ACT.Sqrt, bias=EPS)
+            scale = small.tile([P, HEAD_TILES], F32, name="scale")
+            nc.vector.reciprocal(out=scale[:], in_=std[:])
+            nc.vector.tensor_mul(out=scale[:], in0=scale[:], in1=gain_shift[:, tiles])
+            shift = small.tile([P, HEAD_TILES], F32, name="shift")
+            nc.vector.tensor_mul(out=shift[:], in0=mean_var[:, :, 0], in1=scale[:])
+            nc.vector.tensor_sub(out=shift[:], in0=gain_shift[:, shifts], in1=shift[:])
+            z = []
+            for t in range(HEAD_TILES):
+                z_t = normed.tile([P, ROWS], F32, name="z_t")
+                for half in range(2):
+                    nc.scalar.activation(
+                        out=z_t[:, half * HALF_ROWS : (half + 1) * HALF_ROWS],
+                        in_=y[2 * t + half][:],
+                        func=ACT.Identity,
+                        scale=scale[:, t : t + 1],
+                        bias=shift[:, t : t + 1],
+                    )
+                z.append(z_t)
+            return z
+
+        def transpose_and_store(h, z):
+            for t in range(HEAD_TILES):
+                rows = result.tile([P, ROW_TILES * P], F32, name="rows")
+                if t == 0:
+                    dest = rows[:].rearrange("p (s j f) -> p s j f", s=2, j=ROW_TILES, f=KD)
+                else:
+                    dest = rows[:].rearrange("p (j f) -> p j f", j=ROW_TILES, f=P)
+                for half in range(2):
+                    bank = t_banks.tile([P, HALF_TILES, P], F32, tag="t", name="rows_bank")
+                    for j in range(HALF_TILES):
+                        first = (half * HALF_TILES + j) * P
+                        nc.tensor.transpose(bank[:, j, :], z[t][:, first : first + P], ident[:])
+                    js = slice(half * HALF_TILES, (half + 1) * HALF_TILES)
+                    if t == 0:
+                        nc.scalar.copy(
+                            out=dest[:, :, js, :],
+                            in_=bank[:].rearrange("p j (s f) -> p s j f", s=2),
+                        )
+                    else:
+                        nc.scalar.copy(out=dest[:, js, :], in_=bank[:])
+                if t == 0:
+                    nc.sync.dma_start(out=q_rows[h], in_=rows[:, 0 : ROW_TILES * KD])
+                    nc.sync.dma_start(out=k_rows[h], in_=rows[:, ROW_TILES * KD :])
+                else:
+                    nc.sync.dma_start(out=v_rows[h], in_=rows[:])
+
+        quantise_x(0)
+        quantise_w(0)
+        quantise_x(1)
+        z_of = {}
+        for h in range(HEADS + 1):
+            if h + 1 < HEADS:
+                quantise_w(h + 1)
+            if h < HEADS:
+                z_of[h] = project_and_normalise(h)
+            if h >= 1:
+                transpose_and_store(h - 1, z_of[h - 1])

@@ -9,6 +9,7 @@ U32 = mybir.dt.uint32
 U8 = mybir.dt.uint8
 FP8X4 = mybir.dt.float8_e4m3fn_x4
 ACT = mybir.ActivationFunctionType
+ALU = mybir.AluOpType
 
 P = 128
 BATCH, TOKENS, DIM = 4, 256, 1024
@@ -23,9 +24,11 @@ PASSES = DIM // 512
 WORDS = DIM // 2
 CHUNKS = WORDS // P
 HEAD_TILES = 2
+N_TILES = HEADS * HEAD_TILES
 TILE_CODES = PASSES * P
+W_LEAD = 3
 
-FLOPS = 2 * ROWS * DIM * HEADS * HEAD_TILES * P
+FLOPS = 2 * ROWS * DIM * N_TILES * P
 
 
 def tile_attention_pa_kernel(tc, x, qkv_w, qkv_g, qkv_b, out_q, out_k, out_v):
@@ -34,17 +37,24 @@ def tile_attention_pa_kernel(tc, x, qkv_w, qkv_g, qkv_b, out_q, out_k, out_v):
         keep = ctx.enter_context(tc.tile_pool(name="keep", bufs=1))
         stage = ctx.enter_context(tc.tile_pool(name="stage", bufs=2))
         small = ctx.enter_context(tc.tile_pool(name="small", bufs=3))
-        normed = ctx.enter_context(tc.tile_pool(name="normed", bufs=2 * HEAD_TILES))
-        result = ctx.enter_context(tc.tile_pool(name="result", bufs=2 * HEAD_TILES))
-        y_banks = ctx.enter_context(tc.psum_pool(name="y_banks", bufs=4))
-        t_banks = ctx.enter_context(tc.psum_pool(name="t_banks", bufs=4))
+        normed = ctx.enter_context(tc.tile_pool(name="normed", bufs=3))
+        result = ctx.enter_context(tc.tile_pool(name="result", bufs=4))
+        y_banks = ctx.enter_context(tc.psum_pool(name="y_banks", bufs=5))
+        t_banks = ctx.enter_context(tc.psum_pool(name="t_banks", bufs=3))
+        ctx.enter_context(tc.manual_schedule())
 
         x_rows = x.rearrange("b (tp j) k -> tp b (j k)", j=ROW_TILES)
         q_rows = out_q.rearrange("b h (tp j) f -> h tp b (j f)", j=ROW_TILES)
         k_rows = out_k.rearrange("b h (tp j) f -> h tp b (j f)", j=ROW_TILES)
         v_rows = out_v.rearrange("b h (tp j) f -> h tp b (j f)", j=ROW_TILES)
-        w_rows = qkv_w.rearrange("(ft m) k -> m ft k", m=P)
+        w_rows = qkv_w.rearrange("(i m) k -> m i k", m=P)
 
+        gb_rows = keep.tile([P, P], BF16, name="gb_rows")
+        nc.vector.memset(gb_rows[:], 0.0)
+        nc.scalar.dma_start(out=gb_rows[0:N_TILES, :], in_=qkv_g.rearrange("(i m) -> i m", m=P))
+        nc.scalar.dma_start(
+            out=gb_rows[32 : 32 + N_TILES, :], in_=qkv_b.rearrange("(i m) -> i m", m=P)
+        )
         x_raw = []
         w_raw = []
         for half in range(2):
@@ -70,44 +80,30 @@ def tile_attention_pa_kernel(tc, x, qkv_w, qkv_g, qkv_b, out_q, out_k, out_v):
 
         ident = keep.tile([P, P], F32, name="ident")
         make_identity(nc, ident[:])
-        one = keep.tile([P, 1], F32, name="one")
-        nc.vector.memset(one[:], 1.0)
-        table_warm = keep.tile([P, 1], F32, name="table_warm")
-        nc.scalar.activation(out=table_warm[:], in_=one[:], func=ACT.Sqrt)
-
-        n_tiles = HEADS * HEAD_TILES
-        gb_rows = keep.tile([P, P], BF16, name="gb_rows")
-        nc.vector.memset(gb_rows[:], 0.0)
-        nc.scalar.dma_start(out=gb_rows[0:n_tiles, :], in_=qkv_g.rearrange("(ft m) -> ft m", m=P))
-        nc.scalar.dma_start(
-            out=gb_rows[32 : 32 + n_tiles, :], in_=qkv_b.rearrange("(ft m) -> ft m", m=P)
-        )
-        gb_rows_f32 = keep.tile([P, P], F32, name="gb_rows_f32")
-        nc.vector.tensor_copy(out=gb_rows_f32[:], in_=gb_rows[:])
-        gb_bank = t_banks.tile([P, CHUNKS, P], F32, tag="t", name="gb_bank")
-        nc.tensor.transpose(gb_bank[:, 0, :], gb_rows_f32[:], ident[:])
-        gain_shift = keep.tile([P, 64], F32, name="gain_shift")
-        nc.vector.tensor_copy(out=gain_shift[:], in_=gb_bank[:, 0, 0:64])
+        minus_half = keep.tile([P, 1], F32, name="minus_half")
+        nc.gpsimd.memset(minus_half[:], -0.5)
 
         x_codes = keep.tile([P, 2 * PASSES * HALF_ROWS], U32, name="x_codes", align_bytes=64)
         x_scales = keep.tile([P, 2 * PASSES * HALF_ROWS], U8, name="x_scales", align_bytes=64)
-        w_codes = keep.tile([P, n_tiles * TILE_CODES], U32, name="w_codes", align_bytes=64)
-        w_scales = keep.tile([P, n_tiles * TILE_CODES], U8, name="w_scales", align_bytes=64)
+        w_codes = keep.tile([P, N_TILES * TILE_CODES], U32, name="w_codes", align_bytes=64)
+        w_scales = keep.tile([P, N_TILES * TILE_CODES], U8, name="w_scales", align_bytes=64)
 
-        def transpose_row_tile(words):
+        def channels_to_partitions(words):
             bank = t_banks.tile([P, CHUNKS, P], F32, tag="t", name="kt_bank")
             for c in range(CHUNKS):
                 nc.tensor.transpose(bank[:, c, :], words[:, c * P : (c + 1) * P], ident[:])
             return bank[:].rearrange("p (g u) r -> p g r u", u=2)
 
         def quantise_x(half):
-            grouped = stage.tile([P, 4 * PASSES * HALF_ROWS], BF16, name="x_grouped", align_bytes=64)
+            grouped = stage.tile(
+                [P, 4 * PASSES * HALF_ROWS], BF16, name="x_grouped", align_bytes=64
+            )
             grouped_words = grouped[:].bitcast(F32).rearrange(
                 "p (g j r u) -> p g j r u", g=PASSES, j=HALF_TILES, r=P, u=2
             )
             words = x_raw[half][:].bitcast(F32)
             for j in range(HALF_TILES):
-                pairs = transpose_row_tile(words[:, j * WORDS : (j + 1) * WORDS])
+                pairs = channels_to_partitions(words[:, j * WORDS : (j + 1) * WORDS])
                 if j % 2 == 0:
                     nc.vector.tensor_copy(out=grouped_words[:, :, j], in_=pairs)
                 else:
@@ -117,107 +113,138 @@ def tile_attention_pa_kernel(tc, x, qkv_w, qkv_g, qkv_b, out_q, out_k, out_v):
                 out=x_codes[:, cols].bitcast(FP8X4), scales=x_scales[:, cols], in_=grouped[:]
             )
 
-        def quantise_w(h):
-            grouped = stage.tile([P, 4 * HEAD_TILES * TILE_CODES], BF16, name="w_grouped", align_bytes=64)
-            grouped_words = grouped[:].bitcast(F32).rearrange(
-                "p (t g m u) -> p t g m u", t=HEAD_TILES, g=PASSES, m=P, u=2
+        w_grouped = {}
+
+        def regroup_w(i):
+            grouped = stage.tile([P, 4 * TILE_CODES], BF16, name="w_grouped", align_bytes=64)
+            words = w_raw[i // HEAD_TILES][:].bitcast(F32)
+            first = (i % HEAD_TILES) * WORDS
+            pairs = channels_to_partitions(words[:, first : first + WORDS])
+            nc.scalar.copy(
+                out=grouped[:].bitcast(F32).rearrange("p (g m u) -> p g m u", g=PASSES, m=P, u=2),
+                in_=pairs,
             )
-            words = w_raw[h][:].bitcast(F32)
-            for t in range(HEAD_TILES):
-                pairs = transpose_row_tile(words[:, t * WORDS : (t + 1) * WORDS])
-                nc.vector.tensor_copy(out=grouped_words[:, t], in_=pairs)
-            cols = slice(h * HEAD_TILES * TILE_CODES, (h + 1) * HEAD_TILES * TILE_CODES)
+            w_grouped[i] = grouped
+
+        def quantise_w(i):
+            cols = slice(i * TILE_CODES, (i + 1) * TILE_CODES)
             nc.vector.quantize_mx(
-                out=w_codes[:, cols].bitcast(FP8X4), scales=w_scales[:, cols], in_=grouped[:]
+                out=w_codes[:, cols].bitcast(FP8X4), scales=w_scales[:, cols], in_=w_grouped[i][:]
             )
 
-        def project_and_normalise(h):
-            stats = small.tile([P, HEAD_TILES, 2, 6], F32, name="stats")
-            mean_var = small.tile([P, HEAD_TILES, 2], F32, name="mean_var")
-            y = []
-            for t in range(HEAD_TILES):
-                for half in range(2):
-                    bank = y_banks.tile([P, HALF_ROWS], F32, tag="y", name="y_bank")
-                    for g in range(PASSES):
-                        w_cols = slice(
-                            ((h * HEAD_TILES + t) * PASSES + g) * P,
-                            ((h * HEAD_TILES + t) * PASSES + g + 1) * P,
-                        )
-                        x_cols = slice(
-                            (half * PASSES + g) * HALF_ROWS, (half * PASSES + g + 1) * HALF_ROWS
-                        )
-                        nc.tensor.matmul_mx(
-                            out=bank[:],
-                            lhsT=w_codes[:, w_cols].bitcast(FP8X4),
-                            lhsT_scale=w_scales[:, w_cols],
-                            rhs=x_codes[:, x_cols].bitcast(FP8X4),
-                            rhs_scale=x_scales[:, x_cols],
-                            start=(g == 0),
-                            stop=(g == PASSES - 1),
-                        )
-                    nc.vector.bn_stats(out=stats[:, t, half, :], in_=bank[:])
-                    y.append(bank)
-                nc.vector.bn_aggr(
-                    out=mean_var[:, t, :], in_=stats[:, t].rearrange("p a s -> p (a s)")
-                )
-            tiles = slice(h * HEAD_TILES, (h + 1) * HEAD_TILES)
-            shifts = slice(32 + h * HEAD_TILES, 32 + (h + 1) * HEAD_TILES)
-            std = small.tile([P, HEAD_TILES], F32, name="std")
-            nc.scalar.activation(out=std[:], in_=mean_var[:, :, 1], func=ACT.Sqrt, bias=EPS)
-            scale = small.tile([P, HEAD_TILES], F32, name="scale")
-            nc.vector.reciprocal(out=scale[:], in_=std[:])
-            nc.vector.tensor_mul(out=scale[:], in0=scale[:], in1=gain_shift[:, tiles])
-            shift = small.tile([P, HEAD_TILES], F32, name="shift")
-            nc.vector.tensor_mul(out=shift[:], in0=mean_var[:, :, 0], in1=scale[:])
-            nc.vector.tensor_sub(out=shift[:], in0=gain_shift[:, shifts], in1=shift[:])
-            z = []
-            for t in range(HEAD_TILES):
-                z_t = normed.tile([P, ROWS], F32, name="z_t")
-                for half in range(2):
-                    nc.scalar.activation(
-                        out=z_t[:, half * HALF_ROWS : (half + 1) * HALF_ROWS],
-                        in_=y[2 * t + half][:],
-                        func=ACT.Identity,
-                        scale=scale[:, t : t + 1],
-                        bias=shift[:, t : t + 1],
-                    )
-                z.append(z_t)
-            return z
+        y_of = {}
+        stats_of = {}
+        scale_shift_of = {}
+        z_of = {}
 
-        def transpose_and_store(h, z):
-            for t in range(HEAD_TILES):
-                rows = result.tile([P, ROW_TILES * P], F32, name="rows")
-                if t == 0:
-                    dest = rows[:].rearrange("p (s j f) -> p s j f", s=2, j=ROW_TILES, f=KD)
+        def project(i):
+            stats = small.tile([P, 2, 6], F32, name="stats")
+            y_of[i] = []
+            for half in range(2):
+                bank = y_banks.tile([P, HALF_ROWS], F32, tag="y", name="y_bank")
+                for g in range(PASSES):
+                    w_cols = slice((i * PASSES + g) * P, (i * PASSES + g + 1) * P)
+                    x_cols = slice(
+                        (half * PASSES + g) * HALF_ROWS, (half * PASSES + g + 1) * HALF_ROWS
+                    )
+                    nc.tensor.matmul_mx(
+                        out=bank[:],
+                        lhsT=w_codes[:, w_cols].bitcast(FP8X4),
+                        lhsT_scale=w_scales[:, w_cols],
+                        rhs=x_codes[:, x_cols].bitcast(FP8X4),
+                        rhs_scale=x_scales[:, x_cols],
+                        start=(g == 0),
+                        stop=(g == PASSES - 1),
+                    )
+                nc.vector.bn_stats(out=stats[:, half, :], in_=bank[:])
+                y_of[i].append(bank)
+            stats_of[i] = stats
+
+        def scale_and_shift(i):
+            mean_var = small.tile([P, 2], F32, name="mean_var")
+            nc.vector.bn_aggr(out=mean_var[:], in_=stats_of[i][:].rearrange("p a s -> p (a s)"))
+            chain = small.tile([P, 5], F32, name="chain")
+            nc.gpsimd.tensor_scalar(
+                out=chain[:, 0:1], in0=mean_var[:, 1:2], scalar1=1.0, scalar2=EPS,
+                op0=ALU.mult, op1=ALU.add,
+            )
+            nc.gpsimd.tensor_tensor(
+                out=chain[:, 1:2], in0=chain[:, 0:1], in1=minus_half[:], op=ALU.pow
+            )
+            nc.gpsimd.tensor_mul(out=chain[:, 2:3], in0=chain[:, 1:2], in1=gain[:, i : i + 1])
+            nc.gpsimd.tensor_mul(out=chain[:, 3:4], in0=chain[:, 1:2], in1=neg_gain[:, i : i + 1])
+            nc.gpsimd.tensor_scalar(
+                out=chain[:, 4:5], in0=mean_var[:, 0:1], scalar1=chain[:, 3:4],
+                scalar2=shift_in[:, i : i + 1], op0=ALU.mult, op1=ALU.add,
+            )
+            scale_shift_of[i] = (chain[:, 2:3], chain[:, 4:5])
+
+        def normalise(i):
+            scale, shift = scale_shift_of[i]
+            z_t = normed.tile([P, ROWS], F32, name="z_t")
+            nc.scalar.activation(
+                out=z_t[:, 0:HALF_ROWS], in_=y_of[i][0][:], func=ACT.Identity,
+                scale=scale, bias=shift,
+            )
+            nc.vector.tensor_scalar(
+                out=z_t[:, HALF_ROWS:ROWS], in0=y_of[i][1][:], scalar1=scale, scalar2=shift,
+                op0=ALU.mult, op1=ALU.add,
+            )
+            z_of[i] = z_t
+
+        def rows_to_partitions_and_store(i):
+            h = i // HEAD_TILES
+            is_qk = i % HEAD_TILES == 0
+            rows = result.tile([P, ROW_TILES * P], F32, name="rows")
+            for half in range(2):
+                bank = t_banks.tile([P, HALF_TILES, P], F32, tag="t", name="rows_bank")
+                for j in range(HALF_TILES):
+                    first = (half * HALF_TILES + j) * P
+                    nc.tensor.transpose(bank[:, j, :], z_of[i][:, first : first + P], ident[:])
+                js = slice(half * HALF_TILES, (half + 1) * HALF_TILES)
+                if is_qk:
+                    nc.scalar.copy(
+                        out=rows[:].rearrange("p (s j f) -> p s j f", s=2, j=ROW_TILES)[:, :, js, :],
+                        in_=bank[:].rearrange("p j (s f) -> p s j f", s=2),
+                    )
                 else:
-                    dest = rows[:].rearrange("p (j f) -> p j f", j=ROW_TILES, f=P)
-                for half in range(2):
-                    bank = t_banks.tile([P, HALF_TILES, P], F32, tag="t", name="rows_bank")
-                    for j in range(HALF_TILES):
-                        first = (half * HALF_TILES + j) * P
-                        nc.tensor.transpose(bank[:, j, :], z[t][:, first : first + P], ident[:])
-                    js = slice(half * HALF_TILES, (half + 1) * HALF_TILES)
-                    if t == 0:
-                        nc.scalar.copy(
-                            out=dest[:, :, js, :],
-                            in_=bank[:].rearrange("p j (s f) -> p s j f", s=2),
-                        )
-                    else:
-                        nc.scalar.copy(out=dest[:, js, :], in_=bank[:])
-                if t == 0:
-                    nc.sync.dma_start(out=q_rows[h], in_=rows[:, 0 : ROW_TILES * KD])
-                    nc.sync.dma_start(out=k_rows[h], in_=rows[:, ROW_TILES * KD :])
-                else:
-                    nc.sync.dma_start(out=v_rows[h], in_=rows[:])
+                    nc.scalar.copy(
+                        out=rows[:].rearrange("p (j f) -> p j f", j=ROW_TILES)[:, js, :], in_=bank[:]
+                    )
+            if is_qk:
+                nc.sync.dma_start(out=q_rows[h], in_=rows[:, 0 : ROW_TILES * KD])
+                nc.sync.dma_start(out=k_rows[h], in_=rows[:, ROW_TILES * KD :])
+            else:
+                nc.sync.dma_start(out=v_rows[h], in_=rows[:])
 
         quantise_x(0)
-        quantise_w(0)
+        for i in range(W_LEAD):
+            regroup_w(i)
+            if i >= 1:
+                quantise_w(i - 1)
         quantise_x(1)
-        z_of = {}
-        for h in range(HEADS + 1):
-            if h + 1 < HEADS:
-                quantise_w(h + 1)
-            if h < HEADS:
-                z_of[h] = project_and_normalise(h)
-            if h >= 1:
-                transpose_and_store(h - 1, z_of[h - 1])
+
+        gb_rows_f32 = keep.tile([P, P], F32, name="gb_rows_f32")
+        nc.vector.tensor_copy(out=gb_rows_f32[:], in_=gb_rows[:])
+        gb_bank = t_banks.tile([P, CHUNKS, P], F32, tag="t", name="gb_bank")
+        nc.tensor.transpose(gb_bank[:, 0, :], gb_rows_f32[:], ident[:])
+        gain = keep.tile([P, N_TILES], F32, name="gain")
+        neg_gain = keep.tile([P, N_TILES], F32, name="neg_gain")
+        shift_in = keep.tile([P, N_TILES], F32, name="shift_in")
+        nc.vector.tensor_copy(out=gain[:], in_=gb_bank[:, 0, 0:N_TILES])
+        nc.vector.tensor_scalar_mul(out=neg_gain[:], in0=gb_bank[:, 0, 0:N_TILES], scalar1=-1.0)
+        nc.vector.tensor_copy(out=shift_in[:], in_=gb_bank[:, 0, 32 : 32 + N_TILES])
+
+        for i in range(N_TILES + 2):
+            if i < N_TILES:
+                project(i)
+            if i + W_LEAD - 1 < N_TILES:
+                quantise_w(i + W_LEAD - 1)
+            if i < N_TILES:
+                scale_and_shift(i)
+            if 0 <= i - 1 < N_TILES:
+                normalise(i - 1)
+            if i + W_LEAD < N_TILES:
+                regroup_w(i + W_LEAD)
+            if i >= 2:
+                rows_to_partitions_and_store(i - 2)

@@ -26,6 +26,7 @@ CHUNKS = WORDS // P
 HEAD_TILES = 2
 N_TILES = HEADS * HEAD_TILES
 TILE_CODES = PASSES * P
+X_LOADS = 4
 W_LEAD = 3
 
 FLOPS = 2 * ROWS * DIM * N_TILES * P
@@ -55,16 +56,18 @@ def tile_attention_pa_kernel(tc, x, qkv_w, qkv_g, qkv_b, out_q, out_k, out_v):
         nc.scalar.dma_start(
             out=gb_rows[32 : 32 + N_TILES, :], in_=qkv_b.rearrange("(i m) -> i m", m=P)
         )
+        x_load_cols = ROW_TILES * DIM // X_LOADS
         x_raw = []
         w_raw = []
-        for half in range(2):
-            x_raw.append(keep.tile([P, HALF_TILES * DIM], BF16, name="x_raw%d" % half))
+        for n in range(X_LOADS):
+            x_raw.append(keep.tile([P, x_load_cols], BF16, name="x_raw%d" % n))
         for h in range(HEADS):
             w_raw.append(keep.tile([P, HEAD_TILES * DIM], BF16, name="w_raw%d" % h))
 
-        def load_x(half):
-            cols = slice(half * HALF_TILES * DIM, (half + 1) * HALF_TILES * DIM)
-            nc.sync.dma_start(out=x_raw[half][:], in_=x_rows[:, :, cols])
+        def load_x(n):
+            nc.sync.dma_start(
+                out=x_raw[n][:], in_=x_rows[:, :, n * x_load_cols : (n + 1) * x_load_cols]
+            )
 
         def load_w(h):
             nc.sync.dma_start(
@@ -73,15 +76,19 @@ def tile_attention_pa_kernel(tc, x, qkv_w, qkv_g, qkv_b, out_q, out_k, out_v):
             )
 
         load_x(0)
-        load_w(0)
         load_x(1)
+        load_w(0)
+        load_x(2)
+        load_x(3)
         for h in range(1, HEADS):
             load_w(h)
 
         ident = keep.tile([P, P], F32, name="ident")
         make_identity(nc, ident[:])
-        minus_half = keep.tile([P, 1], F32, name="minus_half")
-        nc.gpsimd.memset(minus_half[:], -0.5)
+        one = keep.tile([P, 1], F32, name="one")
+        nc.vector.memset(one[:], 1.0)
+        table_warm = keep.tile([P, 1], F32, name="table_warm")
+        nc.scalar.activation(out=table_warm[:], in_=one[:], func=ACT.Abs_reciprocal_sqrt)
 
         x_codes = keep.tile([P, 2 * PASSES * HALF_ROWS], U32, name="x_codes", align_bytes=64)
         x_scales = keep.tile([P, 2 * PASSES * HALF_ROWS], U8, name="x_scales", align_bytes=64)
@@ -101,17 +108,23 @@ def tile_attention_pa_kernel(tc, x, qkv_w, qkv_g, qkv_b, out_q, out_k, out_v):
             grouped_words = grouped[:].bitcast(F32).rearrange(
                 "p (g j r u) -> p g j r u", g=PASSES, j=HALF_TILES, r=P, u=2
             )
-            words = x_raw[half][:].bitcast(F32)
+            tiles_a_load = ROW_TILES // X_LOADS
             for j in range(HALF_TILES):
-                pairs = channels_to_partitions(words[:, j * WORDS : (j + 1) * WORDS])
+                row_tile = half * HALF_TILES + j
+                words = x_raw[row_tile // tiles_a_load][:].bitcast(F32)
+                first = (row_tile % tiles_a_load) * WORDS
+                pairs = channels_to_partitions(words[:, first : first + WORDS])
                 if j % 2 == 0:
                     nc.vector.tensor_copy(out=grouped_words[:, :, j], in_=pairs)
                 else:
                     nc.scalar.copy(out=grouped_words[:, :, j], in_=pairs)
-            cols = slice(half * PASSES * HALF_ROWS, (half + 1) * PASSES * HALF_ROWS)
-            nc.vector.quantize_mx(
-                out=x_codes[:, cols].bitcast(FP8X4), scales=x_scales[:, cols], in_=grouped[:]
-            )
+            for g in range(PASSES):
+                cols = slice((half * PASSES + g) * HALF_ROWS, (half * PASSES + g + 1) * HALF_ROWS)
+                nc.vector.quantize_mx(
+                    out=x_codes[:, cols].bitcast(FP8X4),
+                    scales=x_scales[:, cols],
+                    in_=grouped[:, 4 * g * HALF_ROWS : 4 * (g + 1) * HALF_ROWS],
+                )
 
         w_grouped = {}
 
@@ -134,65 +147,70 @@ def tile_attention_pa_kernel(tc, x, qkv_w, qkv_g, qkv_b, out_q, out_k, out_v):
 
         y_of = {}
         stats_of = {}
-        scale_shift_of = {}
+        mean_var_of = {}
+        rstd_of = {}
+        scales_of = {}
+        shift_of = {}
         z_of = {}
 
-        def project(i):
-            stats = small.tile([P, 2, 6], F32, name="stats")
-            y_of[i] = []
-            for half in range(2):
-                bank = y_banks.tile([P, HALF_ROWS], F32, tag="y", name="y_bank")
-                for g in range(PASSES):
-                    w_cols = slice((i * PASSES + g) * P, (i * PASSES + g + 1) * P)
-                    x_cols = slice(
-                        (half * PASSES + g) * HALF_ROWS, (half * PASSES + g + 1) * HALF_ROWS
-                    )
-                    nc.tensor.matmul_mx(
-                        out=bank[:],
-                        lhsT=w_codes[:, w_cols].bitcast(FP8X4),
-                        lhsT_scale=w_scales[:, w_cols],
-                        rhs=x_codes[:, x_cols].bitcast(FP8X4),
-                        rhs_scale=x_scales[:, x_cols],
-                        start=(g == 0),
-                        stop=(g == PASSES - 1),
-                    )
-                nc.vector.bn_stats(out=stats[:, half, :], in_=bank[:])
-                y_of[i].append(bank)
-            stats_of[i] = stats
+        def project(i, half):
+            if half == 0:
+                stats_of[i] = small.tile([P, 2, 6], F32, name="stats")
+                y_of[i] = []
+            bank = y_banks.tile([P, HALF_ROWS], F32, tag="y", name="y_bank")
+            for g in range(PASSES):
+                w_cols = slice((i * PASSES + g) * P, (i * PASSES + g + 1) * P)
+                x_cols = slice((half * PASSES + g) * HALF_ROWS, (half * PASSES + g + 1) * HALF_ROWS)
+                nc.tensor.matmul_mx(
+                    out=bank[:],
+                    lhsT=w_codes[:, w_cols].bitcast(FP8X4),
+                    lhsT_scale=w_scales[:, w_cols],
+                    rhs=x_codes[:, x_cols].bitcast(FP8X4),
+                    rhs_scale=x_scales[:, x_cols],
+                    start=(g == 0),
+                    stop=(g == PASSES - 1),
+                )
+            nc.vector.bn_stats(out=stats_of[i][:, half, :], in_=bank[:])
+            y_of[i].append(bank)
 
-        def scale_and_shift(i):
+        def mean_var_rstd(i):
             mean_var = small.tile([P, 2], F32, name="mean_var")
             nc.vector.bn_aggr(out=mean_var[:], in_=stats_of[i][:].rearrange("p a s -> p (a s)"))
-            chain = small.tile([P, 5], F32, name="chain")
-            nc.gpsimd.tensor_scalar(
-                out=chain[:, 0:1], in0=mean_var[:, 1:2], scalar1=1.0, scalar2=EPS,
-                op0=ALU.mult, op1=ALU.add,
+            rstd = small.tile([P, 1], F32, name="rstd")
+            nc.scalar.activation(
+                out=rstd[:], in_=mean_var[:, 1:2], func=ACT.Abs_reciprocal_sqrt, bias=EPS
             )
-            nc.gpsimd.tensor_tensor(
-                out=chain[:, 1:2], in0=chain[:, 0:1], in1=minus_half[:], op=ALU.pow
+            mean_var_of[i] = mean_var
+            rstd_of[i] = rstd
+
+        def compute_scales(i):
+            both = small.tile([P, 2], F32, name="scales")
+            nc.vector.tensor_scalar_mul(
+                out=both[:], in0=gain_pm[:, i, :], scalar1=rstd_of[i][:, 0:1]
             )
-            nc.gpsimd.tensor_mul(out=chain[:, 2:3], in0=chain[:, 1:2], in1=gain[:, i : i + 1])
-            nc.gpsimd.tensor_mul(out=chain[:, 3:4], in0=chain[:, 1:2], in1=neg_gain[:, i : i + 1])
-            nc.gpsimd.tensor_scalar(
-                out=chain[:, 4:5], in0=mean_var[:, 0:1], scalar1=chain[:, 3:4],
+            scales_of[i] = both
+
+        def compute_shift(i):
+            shift_i = small.tile([P, 1], F32, name="shift")
+            nc.vector.tensor_scalar(
+                out=shift_i[:], in0=mean_var_of[i][:, 0:1], scalar1=scales_of[i][:, 1:2],
                 scalar2=shift_in[:, i : i + 1], op0=ALU.mult, op1=ALU.add,
             )
-            scale_shift_of[i] = (chain[:, 2:3], chain[:, 4:5])
+            shift_of[i] = shift_i
 
         def normalise(i):
-            scale, shift = scale_shift_of[i]
             z_t = normed.tile([P, ROWS], F32, name="z_t")
             nc.scalar.activation(
                 out=z_t[:, 0:HALF_ROWS], in_=y_of[i][0][:], func=ACT.Identity,
-                scale=scale, bias=shift,
+                scale=scales_of[i][:, 0:1], bias=shift_of[i][:, 0:1],
             )
             nc.vector.tensor_scalar(
-                out=z_t[:, HALF_ROWS:ROWS], in0=y_of[i][1][:], scalar1=scale, scalar2=shift,
-                op0=ALU.mult, op1=ALU.add,
+                out=z_t[:, HALF_ROWS:ROWS], in0=y_of[i][1][:], scalar1=scales_of[i][:, 0:1],
+                scalar2=shift_of[i][:, 0:1], op0=ALU.mult, op1=ALU.add,
             )
             z_of[i] = z_t
 
-        def rows_to_partitions_and_store(i):
+        def rows_to_partitions_and_store(i, vector_is_free):
             h = i // HEAD_TILES
             is_qk = i % HEAD_TILES == 0
             rows = result.tile([P, ROW_TILES * P], F32, name="rows")
@@ -203,48 +221,58 @@ def tile_attention_pa_kernel(tc, x, qkv_w, qkv_g, qkv_b, out_q, out_k, out_v):
                     nc.tensor.transpose(bank[:, j, :], z_of[i][:, first : first + P], ident[:])
                 js = slice(half * HALF_TILES, (half + 1) * HALF_TILES)
                 if is_qk:
-                    nc.scalar.copy(
-                        out=rows[:].rearrange("p (s j f) -> p s j f", s=2, j=ROW_TILES)[:, :, js, :],
-                        in_=bank[:].rearrange("p j (s f) -> p s j f", s=2),
-                    )
+                    dest = rows[:].rearrange("p (s j f) -> p s j f", s=2, j=ROW_TILES)[:, :, js, :]
+                    source = bank[:].rearrange("p j (s f) -> p s j f", s=2)
                 else:
-                    nc.scalar.copy(
-                        out=rows[:].rearrange("p (j f) -> p j f", j=ROW_TILES)[:, js, :], in_=bank[:]
-                    )
+                    dest = rows[:].rearrange("p (j f) -> p j f", j=ROW_TILES)[:, js, :]
+                    source = bank[:]
+                if vector_is_free and half == 1:
+                    nc.vector.tensor_copy(out=dest, in_=source)
+                else:
+                    nc.scalar.copy(out=dest, in_=source)
+                if not is_qk:
+                    cols = slice(half * HALF_ROWS, (half + 1) * HALF_ROWS)
+                    nc.sync.dma_start(out=v_rows[h][:, :, cols], in_=rows[:, cols])
             if is_qk:
                 nc.sync.dma_start(out=q_rows[h], in_=rows[:, 0 : ROW_TILES * KD])
                 nc.sync.dma_start(out=k_rows[h], in_=rows[:, ROW_TILES * KD :])
-            else:
-                nc.sync.dma_start(out=v_rows[h], in_=rows[:])
 
         quantise_x(0)
-        for i in range(W_LEAD):
-            regroup_w(i)
-            if i >= 1:
-                quantise_w(i - 1)
-        quantise_x(1)
+        regroup_w(0)
+        regroup_w(1)
+        quantise_w(0)
 
         gb_rows_f32 = keep.tile([P, P], F32, name="gb_rows_f32")
         nc.vector.tensor_copy(out=gb_rows_f32[:], in_=gb_rows[:])
         gb_bank = t_banks.tile([P, CHUNKS, P], F32, tag="t", name="gb_bank")
         nc.tensor.transpose(gb_bank[:, 0, :], gb_rows_f32[:], ident[:])
-        gain = keep.tile([P, N_TILES], F32, name="gain")
-        neg_gain = keep.tile([P, N_TILES], F32, name="neg_gain")
+        gain_pm = keep.tile([P, N_TILES, 2], F32, name="gain_pm")
         shift_in = keep.tile([P, N_TILES], F32, name="shift_in")
-        nc.vector.tensor_copy(out=gain[:], in_=gb_bank[:, 0, 0:N_TILES])
-        nc.vector.tensor_scalar_mul(out=neg_gain[:], in0=gb_bank[:, 0, 0:N_TILES], scalar1=-1.0)
+        nc.vector.tensor_copy(out=gain_pm[:, :, 0], in_=gb_bank[:, 0, 0:N_TILES])
+        nc.vector.tensor_scalar_mul(out=gain_pm[:, :, 1], in0=gb_bank[:, 0, 0:N_TILES], scalar1=-1.0)
         nc.vector.tensor_copy(out=shift_in[:], in_=gb_bank[:, 0, 32 : 32 + N_TILES])
 
+        quantise_x(1)
+        quantise_w(1)
+        regroup_w(2)
+
         for i in range(N_TILES + 2):
-            if i < N_TILES:
-                project(i)
-            if i + W_LEAD - 1 < N_TILES:
-                quantise_w(i + W_LEAD - 1)
-            if i < N_TILES:
-                scale_and_shift(i)
+            enters = i < N_TILES
+            if enters:
+                project(i, 0)
+            if 0 <= i - 1 < N_TILES:
+                compute_shift(i - 1)
+            if enters:
+                project(i, 1)
             if 0 <= i - 1 < N_TILES:
                 normalise(i - 1)
+            if enters:
+                mean_var_rstd(i)
+            if i + W_LEAD - 1 < N_TILES:
+                quantise_w(i + W_LEAD - 1)
+            if enters:
+                compute_scales(i)
             if i + W_LEAD < N_TILES:
                 regroup_w(i + W_LEAD)
             if i >= 2:
-                rows_to_partitions_and_store(i - 2)
+                rows_to_partitions_and_store(i - 2, vector_is_free=not enters)

@@ -38,10 +38,11 @@ def tile_attention_pa_kernel(tc, x, qkv_w, qkv_g, qkv_b, out_q, out_k, out_v):
         keep = ctx.enter_context(tc.tile_pool(name="keep", bufs=1))
         stage = ctx.enter_context(tc.tile_pool(name="stage", bufs=2))
         small = ctx.enter_context(tc.tile_pool(name="small", bufs=3))
+        copied = ctx.enter_context(tc.tile_pool(name="copied", bufs=3))
         normed = ctx.enter_context(tc.tile_pool(name="normed", bufs=3))
         result = ctx.enter_context(tc.tile_pool(name="result", bufs=4))
-        y_banks = ctx.enter_context(tc.psum_pool(name="y_banks", bufs=5))
-        t_banks = ctx.enter_context(tc.psum_pool(name="t_banks", bufs=3))
+        y_banks = ctx.enter_context(tc.psum_pool(name="y_banks", bufs=4))
+        t_banks = ctx.enter_context(tc.psum_pool(name="t_banks", bufs=4))
         ctx.enter_context(tc.manual_schedule())
 
         x_rows = x.rearrange("b (tp j) k -> tp b (j k)", j=ROW_TILES)
@@ -146,6 +147,7 @@ def tile_attention_pa_kernel(tc, x, qkv_w, qkv_g, qkv_b, out_q, out_k, out_v):
             )
 
         y_of = {}
+        y_copy_of = {}
         stats_of = {}
         mean_var_of = {}
         rstd_of = {}
@@ -172,6 +174,10 @@ def tile_attention_pa_kernel(tc, x, qkv_w, qkv_g, qkv_b, out_q, out_k, out_v):
                 )
             nc.vector.bn_stats(out=stats_of[i][:, half, :], in_=bank[:])
             y_of[i].append(bank)
+            if half == 0:
+                y_copy = copied.tile([P, HALF_ROWS], F32, name="y_copy")
+                nc.scalar.copy(out=y_copy[:], in_=bank[:])
+                y_copy_of[i] = y_copy
 
         def mean_var_rstd(i):
             mean_var = small.tile([P, 2], F32, name="mean_var")
@@ -199,26 +205,26 @@ def tile_attention_pa_kernel(tc, x, qkv_w, qkv_g, qkv_b, out_q, out_k, out_v):
             shift_of[i] = shift_i
 
         def normalise(i):
-            z_t = normed.tile([P, ROWS], F32, name="z_t")
-            nc.scalar.activation(
-                out=z_t[:, 0:HALF_ROWS], in_=y_of[i][0][:], func=ACT.Identity,
-                scale=scales_of[i][:, 0:1], bias=shift_of[i][:, 0:1],
-            )
+            z_first = normed.tile([P, HALF_ROWS], F32, name="z_first")
+            z_second = normed.tile([P, HALF_ROWS], F32, name="z_second")
             nc.vector.tensor_scalar(
-                out=z_t[:, HALF_ROWS:ROWS], in0=y_of[i][1][:], scalar1=scales_of[i][:, 0:1],
+                out=z_second[:], in0=y_of[i][1][:], scalar1=scales_of[i][:, 0:1],
                 scalar2=shift_of[i][:, 0:1], op0=ALU.mult, op1=ALU.add,
             )
-            z_of[i] = z_t
+            nc.gpsimd.tensor_scalar(
+                out=z_first[:], in0=y_copy_of[i][:], scalar1=scales_of[i][:, 0:1],
+                scalar2=shift_of[i][:, 0:1], op0=ALU.mult, op1=ALU.add,
+            )
+            z_of[i] = (z_first, z_second)
 
         def rows_to_partitions_and_store(i, vector_is_free):
             h = i // HEAD_TILES
             is_qk = i % HEAD_TILES == 0
             rows = result.tile([P, ROW_TILES * P], F32, name="rows")
-            for half in range(2):
+            for half in (1, 0):
                 bank = t_banks.tile([P, HALF_TILES, P], F32, tag="t", name="rows_bank")
                 for j in range(HALF_TILES):
-                    first = (half * HALF_TILES + j) * P
-                    nc.tensor.transpose(bank[:, j, :], z_of[i][:, first : first + P], ident[:])
+                    nc.tensor.transpose(bank[:, j, :], z_of[i][half][:, j * P : (j + 1) * P], ident[:])
                 js = slice(half * HALF_TILES, (half + 1) * HALF_TILES)
                 if is_qk:
                     dest = rows[:].rearrange("p (s j f) -> p s j f", s=2, j=ROW_TILES)[:, :, js, :]
@@ -226,7 +232,7 @@ def tile_attention_pa_kernel(tc, x, qkv_w, qkv_g, qkv_b, out_q, out_k, out_v):
                 else:
                     dest = rows[:].rearrange("p (j f) -> p j f", j=ROW_TILES)[:, js, :]
                     source = bank[:]
-                if vector_is_free and half == 1:
+                if vector_is_free and half == 0:
                     nc.vector.tensor_copy(out=dest, in_=source)
                 else:
                     nc.scalar.copy(out=dest, in_=source)

@@ -43,7 +43,6 @@ def tile_attention_pa_kernel(tc, x, qkv_w, qkv_g, qkv_b, out_q, out_k, out_v):
         result = ctx.enter_context(tc.tile_pool(name="result", bufs=4))
         y_banks = ctx.enter_context(tc.psum_pool(name="y_banks", bufs=4))
         t_banks = ctx.enter_context(tc.psum_pool(name="t_banks", bufs=4))
-        ctx.enter_context(tc.manual_schedule())
 
         x_rows = x.rearrange("b (tp j) k -> tp b (j k)", j=ROW_TILES)
         q_rows = out_q.rearrange("b h (tp j) f -> h tp b (j f)", j=ROW_TILES)

@@ -12,6 +12,8 @@ ACT = mybir.ActivationFunctionType
 ALU = mybir.AluOpType
 
 P = 128
+PACK = 4
+BN_STATS_DIM = 6
 BATCH, TOKENS, DIM = 4, 256, 1024
 HEADS, KD = 12, 64
 EPS = 1e-5
@@ -20,12 +22,13 @@ ROWS = BATCH * TOKENS
 ROW_TILES = ROWS // P
 HALF_TILES = ROW_TILES // 2
 HALF_ROWS = HALF_TILES * P
-PASSES = DIM // 512
-WORDS = DIM // 2
-CHUNKS = WORDS // P
+PASSES = DIM // (P * PACK)
+PAIRS = DIM // 2
+CHUNKS = PAIRS // P
 HEAD_TILES = 2
 N_TILES = HEADS * HEAD_TILES
-TILE_CODES = PASSES * P
+TILE_WORDS = PASSES * P
+SHIFT_ROW = 32
 X_LOADS = 4
 W_LEAD = 3
 
@@ -43,6 +46,7 @@ def tile_attention_pa_kernel(tc, x, qkv_w, qkv_g, qkv_b, out_q, out_k, out_v):
         result = ctx.enter_context(tc.tile_pool(name="result", bufs=4))
         y_banks = ctx.enter_context(tc.psum_pool(name="y_banks", bufs=4))
         t_banks = ctx.enter_context(tc.psum_pool(name="t_banks", bufs=4))
+        ctx.enter_context(tc.manual_schedule())
 
         x_rows = x.rearrange("b (tp j) k -> tp b (j k)", j=ROW_TILES)
         q_rows = out_q.rearrange("b h (tp j) f -> h tp b (j f)", j=ROW_TILES)
@@ -54,7 +58,8 @@ def tile_attention_pa_kernel(tc, x, qkv_w, qkv_g, qkv_b, out_q, out_k, out_v):
         nc.vector.memset(gb_rows[:], 0.0)
         nc.scalar.dma_start(out=gb_rows[0:N_TILES, :], in_=qkv_g.rearrange("(i m) -> i m", m=P))
         nc.scalar.dma_start(
-            out=gb_rows[32 : 32 + N_TILES, :], in_=qkv_b.rearrange("(i m) -> i m", m=P)
+            out=gb_rows[SHIFT_ROW : SHIFT_ROW + N_TILES, :],
+            in_=qkv_b.rearrange("(i m) -> i m", m=P),
         )
         x_load_cols = ROW_TILES * DIM // X_LOADS
         x_raw = []
@@ -92,55 +97,55 @@ def tile_attention_pa_kernel(tc, x, qkv_w, qkv_g, qkv_b, out_q, out_k, out_v):
 
         x_codes = keep.tile([P, 2 * PASSES * HALF_ROWS], U32, name="x_codes", align_bytes=64)
         x_scales = keep.tile([P, 2 * PASSES * HALF_ROWS], U8, name="x_scales", align_bytes=64)
-        w_codes = keep.tile([P, N_TILES * TILE_CODES], U32, name="w_codes", align_bytes=64)
-        w_scales = keep.tile([P, N_TILES * TILE_CODES], U8, name="w_scales", align_bytes=64)
+        w_codes = keep.tile([P, N_TILES * TILE_WORDS], U32, name="w_codes", align_bytes=64)
+        w_scales = keep.tile([P, N_TILES * TILE_WORDS], U8, name="w_scales", align_bytes=64)
 
-        def channels_to_partitions(words):
+        def channels_to_partitions(pairs):
             bank = t_banks.tile([P, CHUNKS, P], F32, tag="t", name="kt_bank")
             for c in range(CHUNKS):
-                nc.tensor.transpose(bank[:, c, :], words[:, c * P : (c + 1) * P], ident[:])
+                nc.tensor.transpose(bank[:, c, :], pairs[:, c * P : (c + 1) * P], ident[:])
             return bank[:].rearrange("p (g u) r -> p g r u", u=2)
 
         def quantise_x(half):
             grouped = stage.tile(
-                [P, 4 * PASSES * HALF_ROWS], BF16, name="x_grouped", align_bytes=64
+                [P, PACK * PASSES * HALF_ROWS], BF16, name="x_grouped", align_bytes=64
             )
-            grouped_words = grouped[:].bitcast(F32).rearrange(
+            grouped_pairs = grouped[:].bitcast(F32).rearrange(
                 "p (g j r u) -> p g j r u", g=PASSES, j=HALF_TILES, r=P, u=2
             )
             tiles_a_load = ROW_TILES // X_LOADS
             for j in range(HALF_TILES):
                 row_tile = half * HALF_TILES + j
-                words = x_raw[row_tile // tiles_a_load][:].bitcast(F32)
-                first = (row_tile % tiles_a_load) * WORDS
-                pairs = channels_to_partitions(words[:, first : first + WORDS])
+                pairs = x_raw[row_tile // tiles_a_load][:].bitcast(F32)
+                first = (row_tile % tiles_a_load) * PAIRS
+                side_by_side = channels_to_partitions(pairs[:, first : first + PAIRS])
                 if j % 2 == 0:
-                    nc.vector.tensor_copy(out=grouped_words[:, :, j], in_=pairs)
+                    nc.vector.tensor_copy(out=grouped_pairs[:, :, j], in_=side_by_side)
                 else:
-                    nc.scalar.copy(out=grouped_words[:, :, j], in_=pairs)
+                    nc.scalar.copy(out=grouped_pairs[:, :, j], in_=side_by_side)
             for g in range(PASSES):
                 cols = slice((half * PASSES + g) * HALF_ROWS, (half * PASSES + g + 1) * HALF_ROWS)
                 nc.vector.quantize_mx(
                     out=x_codes[:, cols].bitcast(FP8X4),
                     scales=x_scales[:, cols],
-                    in_=grouped[:, 4 * g * HALF_ROWS : 4 * (g + 1) * HALF_ROWS],
+                    in_=grouped[:, PACK * g * HALF_ROWS : PACK * (g + 1) * HALF_ROWS],
                 )
 
         w_grouped = {}
 
         def regroup_w(i):
-            grouped = stage.tile([P, 4 * TILE_CODES], BF16, name="w_grouped", align_bytes=64)
-            words = w_raw[i // HEAD_TILES][:].bitcast(F32)
-            first = (i % HEAD_TILES) * WORDS
-            pairs = channels_to_partitions(words[:, first : first + WORDS])
+            grouped = stage.tile([P, PACK * TILE_WORDS], BF16, name="w_grouped", align_bytes=64)
+            pairs = w_raw[i // HEAD_TILES][:].bitcast(F32)
+            first = (i % HEAD_TILES) * PAIRS
+            side_by_side = channels_to_partitions(pairs[:, first : first + PAIRS])
             nc.scalar.copy(
                 out=grouped[:].bitcast(F32).rearrange("p (g m u) -> p g m u", g=PASSES, m=P, u=2),
-                in_=pairs,
+                in_=side_by_side,
             )
             w_grouped[i] = grouped
 
         def quantise_w(i):
-            cols = slice(i * TILE_CODES, (i + 1) * TILE_CODES)
+            cols = slice(i * TILE_WORDS, (i + 1) * TILE_WORDS)
             nc.vector.quantize_mx(
                 out=w_codes[:, cols].bitcast(FP8X4), scales=w_scales[:, cols], in_=w_grouped[i][:]
             )
@@ -156,7 +161,7 @@ def tile_attention_pa_kernel(tc, x, qkv_w, qkv_g, qkv_b, out_q, out_k, out_v):
 
         def project(i, half):
             if half == 0:
-                stats_of[i] = small.tile([P, 2, 6], F32, name="stats")
+                stats_of[i] = small.tile([P, 2, BN_STATS_DIM], F32, name="stats")
                 y_of[i] = []
             bank = y_banks.tile([P, HALF_ROWS], F32, tag="y", name="y_bank")
             for g in range(PASSES):
@@ -242,21 +247,25 @@ def tile_attention_pa_kernel(tc, x, qkv_w, qkv_g, qkv_b, out_q, out_k, out_v):
                 nc.sync.dma_start(out=q_rows[h], in_=rows[:, 0 : ROW_TILES * KD])
                 nc.sync.dma_start(out=k_rows[h], in_=rows[:, ROW_TILES * KD :])
 
+        gb_rows_f32 = keep.tile([P, P], F32, name="gb_rows_f32")
+        gain_pm = keep.tile([P, N_TILES, 2], F32, name="gain_pm")
+        shift_in = keep.tile([P, N_TILES], F32, name="shift_in")
+
+        def turn_gain_and_shift():
+            gb_bank = t_banks.tile([P, CHUNKS, P], F32, tag="t", name="gb_bank")
+            nc.tensor.transpose(gb_bank[:, 0, :], gb_rows_f32[:], ident[:])
+            gains = gb_bank[:, 0, 0:N_TILES]
+            nc.vector.tensor_copy(out=gain_pm[:, :, 0], in_=gains)
+            nc.vector.tensor_scalar_mul(out=gain_pm[:, :, 1], in0=gains, scalar1=-1.0)
+            nc.vector.tensor_copy(
+                out=shift_in[:], in_=gb_bank[:, 0, SHIFT_ROW : SHIFT_ROW + N_TILES]
+            )
+
         quantise_x(0)
+        nc.vector.tensor_copy(out=gb_rows_f32[:], in_=gb_rows[:])
         regroup_w(0)
         regroup_w(1)
         quantise_w(0)
-
-        gb_rows_f32 = keep.tile([P, P], F32, name="gb_rows_f32")
-        nc.vector.tensor_copy(out=gb_rows_f32[:], in_=gb_rows[:])
-        gb_bank = t_banks.tile([P, CHUNKS, P], F32, tag="t", name="gb_bank")
-        nc.tensor.transpose(gb_bank[:, 0, :], gb_rows_f32[:], ident[:])
-        gain_pm = keep.tile([P, N_TILES, 2], F32, name="gain_pm")
-        shift_in = keep.tile([P, N_TILES], F32, name="shift_in")
-        nc.vector.tensor_copy(out=gain_pm[:, :, 0], in_=gb_bank[:, 0, 0:N_TILES])
-        nc.vector.tensor_scalar_mul(out=gain_pm[:, :, 1], in0=gb_bank[:, 0, 0:N_TILES], scalar1=-1.0)
-        nc.vector.tensor_copy(out=shift_in[:], in_=gb_bank[:, 0, 32 : 32 + N_TILES])
-
         quantise_x(1)
         quantise_w(1)
         regroup_w(2)
@@ -271,6 +280,8 @@ def tile_attention_pa_kernel(tc, x, qkv_w, qkv_g, qkv_b, out_q, out_k, out_v):
                 project(i, 1)
             if 0 <= i - 1 < N_TILES:
                 normalise(i - 1)
+            if i == 0:
+                turn_gain_and_shift()
             if enters:
                 mean_var_rstd(i)
             if i + W_LEAD - 1 < N_TILES:

@@ -195,14 +195,14 @@ def tile_attention_pa_kernel(tc, x, qkv_w, qkv_g, qkv_b, out_q, out_k, out_v):
 
         def compute_scales(i):
             both = small.tile([P, 2], F32, name="scales")
-            nc.vector.tensor_scalar_mul(
+            nc.gpsimd.tensor_scalar_mul(
                 out=both[:], in0=gain_pm[:, i, :], scalar1=rstd_of[i][:, 0:1]
             )
             scales_of[i] = both
 
         def compute_shift(i):
             shift_i = small.tile([P, 1], F32, name="shift")
-            nc.vector.tensor_scalar(
+            nc.gpsimd.tensor_scalar(
                 out=shift_i[:], in0=mean_var_of[i][:, 0:1], scalar1=scales_of[i][:, 1:2],
                 scalar2=shift_in[:, i : i + 1], op0=ALU.mult, op1=ALU.add,
             )

@@ -40,6 +40,7 @@ def tile_attention_pa_kernel(tc, x, qkv_w, qkv_g, qkv_b, out_q, out_k, out_v):
     with ExitStack() as ctx:
         keep = ctx.enter_context(tc.tile_pool(name="keep", bufs=1))
         stage = ctx.enter_context(tc.tile_pool(name="stage", bufs=2))
+        w_stage = ctx.enter_context(tc.tile_pool(name="w_stage", bufs=6))
         small = ctx.enter_context(tc.tile_pool(name="small", bufs=3))
         copied = ctx.enter_context(tc.tile_pool(name="copied", bufs=3))
         normed = ctx.enter_context(tc.tile_pool(name="normed", bufs=3))
@@ -134,7 +135,7 @@ def tile_attention_pa_kernel(tc, x, qkv_w, qkv_g, qkv_b, out_q, out_k, out_v):
         w_grouped = {}
 
         def regroup_w(i):
-            grouped = stage.tile([P, PACK * TILE_WORDS], BF16, name="w_grouped", align_bytes=64)
+            grouped = w_stage.tile([P, PACK * TILE_WORDS], BF16, name="w_grouped", align_bytes=64)
             pairs = w_raw[i // HEAD_TILES][:].bitcast(F32)
             first = (i % HEAD_TILES) * PAIRS
             side_by_side = channels_to_partitions(pairs[:, first : first + PAIRS])
@@ -178,31 +179,35 @@ def tile_attention_pa_kernel(tc, x, qkv_w, qkv_g, qkv_b, out_q, out_k, out_v):
                 )
             nc.vector.bn_stats(out=stats_of[i][:, half, :], in_=bank[:])
             y_of[i].append(bank)
-            if half == 0:
+            if half == 0 and i < N_TILES - 1:
                 y_copy = copied.tile([P, HALF_ROWS], F32, name="y_copy")
                 nc.scalar.copy(out=y_copy[:], in_=bank[:])
                 y_copy_of[i] = y_copy
 
-        def mean_var_rstd(i):
+        def aggregate(i):
             mean_var = small.tile([P, 2], F32, name="mean_var")
             nc.vector.bn_aggr(out=mean_var[:], in_=stats_of[i][:].rearrange("p a s -> p (a s)"))
+            mean_var_of[i] = mean_var
+
+        def reciprocal_root(i):
             rstd = small.tile([P, 1], F32, name="rstd")
             nc.scalar.activation(
-                out=rstd[:], in_=mean_var[:, 1:2], func=ACT.Abs_reciprocal_sqrt, bias=EPS
+                out=rstd[:], in_=mean_var_of[i][:, 1:2], func=ACT.Abs_reciprocal_sqrt, bias=EPS
             )
-            mean_var_of[i] = mean_var
             rstd_of[i] = rstd
 
         def compute_scales(i):
             both = small.tile([P, 2], F32, name="scales")
-            nc.gpsimd.tensor_scalar_mul(
+            engine = nc.gpsimd if i < N_TILES - 1 else nc.vector
+            engine.tensor_scalar_mul(
                 out=both[:], in0=gain_pm[:, i, :], scalar1=rstd_of[i][:, 0:1]
             )
             scales_of[i] = both
 
         def compute_shift(i):
             shift_i = small.tile([P, 1], F32, name="shift")
-            nc.gpsimd.tensor_scalar(
+            engine = nc.gpsimd if i < N_TILES - 1 else nc.vector
+            engine.tensor_scalar(
                 out=shift_i[:], in0=mean_var_of[i][:, 0:1], scalar1=scales_of[i][:, 1:2],
                 scalar2=shift_in[:, i : i + 1], op0=ALU.mult, op1=ALU.add,
             )
@@ -215,13 +220,19 @@ def tile_attention_pa_kernel(tc, x, qkv_w, qkv_g, qkv_b, out_q, out_k, out_v):
                 out=z_second[:], in0=y_of[i][1][:], scalar1=scales_of[i][:, 0:1],
                 scalar2=shift_of[i][:, 0:1], op0=ALU.mult, op1=ALU.add,
             )
-            nc.gpsimd.tensor_scalar(
-                out=z_first[:], in0=y_copy_of[i][:], scalar1=scales_of[i][:, 0:1],
-                scalar2=shift_of[i][:, 0:1], op0=ALU.mult, op1=ALU.add,
-            )
+            if i < N_TILES - 1:
+                nc.gpsimd.tensor_scalar(
+                    out=z_first[:], in0=y_copy_of[i][:], scalar1=scales_of[i][:, 0:1],
+                    scalar2=shift_of[i][:, 0:1], op0=ALU.mult, op1=ALU.add,
+                )
+            else:
+                nc.scalar.activation(
+                    out=z_first[:], in_=y_of[i][0][:], func=ACT.Identity,
+                    scale=scales_of[i][:, 0:1], bias=shift_of[i][:, 0:1],
+                )
             z_of[i] = (z_first, z_second)
 
-        def rows_to_partitions_and_store(i, vector_is_free):
+        def rows_to_partitions_and_store(i, vector_is_free, between=None):
             h = i // HEAD_TILES
             is_qk = i % HEAD_TILES == 0
             rows = result.tile([P, ROW_TILES * P], F32, name="rows")
@@ -240,6 +251,8 @@ def tile_attention_pa_kernel(tc, x, qkv_w, qkv_g, qkv_b, out_q, out_k, out_v):
                     nc.vector.tensor_copy(out=dest, in_=source)
                 else:
                     nc.scalar.copy(out=dest, in_=source)
+                if half == 1 and between:
+                    between()
                 if not is_qk:
                     cols = slice(half * HALF_ROWS, (half + 1) * HALF_ROWS)
                     nc.sync.dma_start(out=v_rows[h][:, :, cols], in_=rows[:, cols])
@@ -270,6 +283,8 @@ def tile_attention_pa_kernel(tc, x, qkv_w, qkv_g, qkv_b, out_q, out_k, out_v):
         quantise_w(1)
         regroup_w(2)
 
+        turned = W_LEAD
+        counts = [2, 2]
         for i in range(N_TILES + 2):
             enters = i < N_TILES
             if enters:
@@ -283,12 +298,15 @@ def tile_attention_pa_kernel(tc, x, qkv_w, qkv_g, qkv_b, out_q, out_k, out_v):
             if i == 0:
                 turn_gain_and_shift()
             if enters:
-                mean_var_rstd(i)
+                aggregate(i)
             if i + W_LEAD - 1 < N_TILES:
                 quantise_w(i + W_LEAD - 1)
-            if enters:
+            for n in range(counts[i] if i < len(counts) else 1):
+                if turned < N_TILES:
+                    regroup_w(turned)
+                    turned += 1
+            if i < 2:
+                reciprocal_root(i)
                 compute_scales(i)
-            if i + W_LEAD < N_TILES:
-                regroup_w(i + W_LEAD)
             if i >= 2:
-                rows_to_partitions_and_store(i - 2, vector_is_free=not enters)
+                rows_to_partitions_and_store(i - 2, between=(lambda: (reciprocal_root(i), compute_scales(i))) if enters else None, vector_is_free=not enters)

@@ -40,7 +40,7 @@ def tile_attention_pa_kernel(tc, x, qkv_w, qkv_g, qkv_b, out_q, out_k, out_v):
     with ExitStack() as ctx:
         keep = ctx.enter_context(tc.tile_pool(name="keep", bufs=1))
         stage = ctx.enter_context(tc.tile_pool(name="stage", bufs=2))
-        w_stage = ctx.enter_context(tc.tile_pool(name="w_stage", bufs=6))
+        w_stage = ctx.enter_context(tc.tile_pool(name="w_stage", bufs=8))
         small = ctx.enter_context(tc.tile_pool(name="small", bufs=3))
         copied = ctx.enter_context(tc.tile_pool(name="copied", bufs=3))
         normed = ctx.enter_context(tc.tile_pool(name="normed", bufs=3))
@@ -177,6 +177,9 @@ def tile_attention_pa_kernel(tc, x, qkv_w, qkv_g, qkv_b, out_q, out_k, out_v):
                     start=(g == 0),
                     stop=(g == PASSES - 1),
                 )
+            if i == 0 and half == 0:
+                for n in range(W_LEAD, W_LEAD + 3):
+                    regroup_w(n)
             nc.vector.bn_stats(out=stats_of[i][:, half, :], in_=bank[:])
             y_of[i].append(bank)
             if half == 0 and i < N_TILES - 1:
@@ -283,8 +286,8 @@ def tile_attention_pa_kernel(tc, x, qkv_w, qkv_g, qkv_b, out_q, out_k, out_v):
         quantise_w(1)
         regroup_w(2)
 
-        turned = W_LEAD
-        counts = [2, 2]
+        turned = W_LEAD + 3
+        counts = [1, 2]
         for i in range(N_TILES + 2):
             enters = i < N_TILES
             if enters:

@@ -201,19 +201,29 @@ def tile_attention_pa_kernel(tc, x, qkv_w, qkv_g, qkv_b, out_q, out_k, out_v):
 
         def compute_scales(i):
             both = small.tile([P, 2], F32, name="scales")
-            engine = nc.gpsimd if i < N_TILES - 1 else nc.vector
-            engine.tensor_scalar_mul(
-                out=both[:], in0=gain_pm[:, i, :], scalar1=rstd_of[i][:, 0:1]
-            )
+            if i < N_TILES - 1:
+                nc.gpsimd.tensor_scalar_mul(
+                    out=both[:], in0=gain_pm[:, i, :], scalar1=rstd_of[i][:, 0:1]
+                )
+            else:
+                nc.scalar.activation(
+                    out=both[:], in_=gain_pm[:, i, :], func=ACT.Copy, scale=rstd_of[i][:, 0:1]
+                )
             scales_of[i] = both
 
         def compute_shift(i):
             shift_i = small.tile([P, 1], F32, name="shift")
-            engine = nc.gpsimd if i < N_TILES - 1 else nc.vector
-            engine.tensor_scalar(
-                out=shift_i[:], in0=mean_var_of[i][:, 0:1], scalar1=scales_of[i][:, 1:2],
-                scalar2=shift_in[:, i : i + 1], op0=ALU.mult, op1=ALU.add,
-            )
+            mean = mean_var_of[i][:, 0:1]
+            if i < N_TILES - 1:
+                nc.gpsimd.tensor_scalar(
+                    out=shift_i[:], in0=mean, scalar1=scales_of[i][:, 1:2],
+                    scalar2=shift_in[:, i : i + 1], op0=ALU.mult, op1=ALU.add,
+                )
+            else:
+                nc.scalar.activation(
+                    out=shift_i[:], in_=mean, func=ACT.Identity,
+                    scale=scales_of[i][:, 1:2], bias=shift_in[:, i : i + 1],
+                )
             shift_of[i] = shift_i
 
         def normalise(i):
@@ -292,15 +302,17 @@ def tile_attention_pa_kernel(tc, x, qkv_w, qkv_g, qkv_b, out_q, out_k, out_v):
             enters = i < N_TILES
             if enters:
                 project(i, 0)
-            if 0 <= i - 1 < N_TILES:
+            if 0 <= i - 1 < N_TILES - 1:
                 compute_shift(i - 1)
             if enters:
                 project(i, 1)
-            if 0 <= i - 1 < N_TILES:
+            if i == N_TILES - 1:
+                aggregate(i)
+            if 0 <= i - 1 < N_TILES - 1:
                 normalise(i - 1)
             if i == 0:
                 turn_gain_and_shift()
-            if enters:
+            if i < N_TILES - 1:
                 aggregate(i)
             if i + W_LEAD - 1 < N_TILES:
                 quantise_w(i + W_LEAD - 1)
@@ -312,4 +324,12 @@ def tile_attention_pa_kernel(tc, x, qkv_w, qkv_g, qkv_b, out_q, out_k, out_v):
                 reciprocal_root(i)
                 compute_scales(i)
             if i >= 2:
-                rows_to_partitions_and_store(i - 2, between=(lambda: (reciprocal_root(i), compute_scales(i))) if enters else None, vector_is_free=not enters)
+                if i == N_TILES - 1:
+                    between = lambda: (reciprocal_root(i), compute_scales(i), compute_shift(i))
+                elif enters:
+                    between = lambda: (reciprocal_root(i), compute_scales(i))
+                elif i == N_TILES:
+                    between = lambda: normalise(i - 1)
+                else:
+                    between = None
+                rows_to_partitions_and_store(i - 2, i >= N_TILES - 1, between)

from contextlib import ExitStack

import concourse.mybir as mybir
from concourse.masks import make_identity

F32 = mybir.dt.float32
BF16 = mybir.dt.bfloat16
U32 = mybir.dt.uint32
U8 = mybir.dt.uint8
FP8X4 = mybir.dt.float8_e4m3fn_x4
ACT = mybir.ActivationFunctionType
ALU = mybir.AluOpType

P = 128
PACK = 4
BN_STATS_DIM = 6
BATCH, TOKENS, DIM = 4, 256, 1024
HEADS, KD = 12, 64
EPS = 1e-5

ROWS = BATCH * TOKENS
ROW_TILES = ROWS // P
HALF_TILES = ROW_TILES // 2
HALF_ROWS = HALF_TILES * P
PASSES = DIM // (P * PACK)
PAIRS = DIM // 2
CHUNKS = PAIRS // P
HEAD_TILES = 2
N_TILES = HEADS * HEAD_TILES
TILE_WORDS = PASSES * P
SHIFT_ROW = 32
X_LOADS = 4
W_LEAD = 3

FLOPS = 2 * ROWS * DIM * N_TILES * P


def tile_attention_pa_kernel(tc, x, qkv_w, qkv_g, qkv_b, out_q, out_k, out_v):
    nc = tc.nc
    with ExitStack() as ctx:
        keep = ctx.enter_context(tc.tile_pool(name="keep", bufs=1))
        stage = ctx.enter_context(tc.tile_pool(name="stage", bufs=2))
        w_stage = ctx.enter_context(tc.tile_pool(name="w_stage", bufs=8))
        small = ctx.enter_context(tc.tile_pool(name="small", bufs=3))
        copied = ctx.enter_context(tc.tile_pool(name="copied", bufs=3))
        normed = ctx.enter_context(tc.tile_pool(name="normed", bufs=3))
        result = ctx.enter_context(tc.tile_pool(name="result", bufs=4))
        y_banks = ctx.enter_context(tc.psum_pool(name="y_banks", bufs=4))
        t_banks = ctx.enter_context(tc.psum_pool(name="t_banks", bufs=4))
        ctx.enter_context(tc.manual_schedule())

        x_rows = x.rearrange("b (tp j) k -> tp b (j k)", j=ROW_TILES)
        q_rows = out_q.rearrange("b h (tp j) f -> h tp b (j f)", j=ROW_TILES)
        k_rows = out_k.rearrange("b h (tp j) f -> h tp b (j f)", j=ROW_TILES)
        v_rows = out_v.rearrange("b h (tp j) f -> h tp b (j f)", j=ROW_TILES)
        w_rows = qkv_w.rearrange("(i m) k -> m i k", m=P)

        gb_rows = keep.tile([P, P], BF16, name="gb_rows")
        nc.vector.memset(gb_rows[:], 0.0)
        nc.scalar.dma_start(out=gb_rows[0:N_TILES, :], in_=qkv_g.rearrange("(i m) -> i m", m=P))
        nc.scalar.dma_start(
            out=gb_rows[SHIFT_ROW : SHIFT_ROW + N_TILES, :],
            in_=qkv_b.rearrange("(i m) -> i m", m=P),
        )
        x_load_cols = ROW_TILES * DIM // X_LOADS
        x_raw = []
        w_raw = []
        for n in range(X_LOADS):
            x_raw.append(keep.tile([P, x_load_cols], BF16, name="x_raw%d" % n))
        for h in range(HEADS):
            w_raw.append(keep.tile([P, HEAD_TILES * DIM], BF16, name="w_raw%d" % h))

        def load_x(n):
            nc.sync.dma_start(
                out=x_raw[n][:], in_=x_rows[:, :, n * x_load_cols : (n + 1) * x_load_cols]
            )

        def load_w(h):
            nc.sync.dma_start(
                out=w_raw[h][:].rearrange("p (t k) -> p t k", t=HEAD_TILES),
                in_=w_rows[:, HEAD_TILES * h : HEAD_TILES * (h + 1), :],
            )

        load_x(0)
        load_x(1)
        load_w(0)
        load_x(2)
        load_x(3)
        for h in range(1, HEADS):
            load_w(h)

        ident = keep.tile([P, P], F32, name="ident")
        make_identity(nc, ident[:])
        one = keep.tile([P, 1], F32, name="one")
        nc.vector.memset(one[:], 1.0)
        table_warm = keep.tile([P, 1], F32, name="table_warm")
        nc.scalar.activation(out=table_warm[:], in_=one[:], func=ACT.Abs_reciprocal_sqrt)

        x_codes = keep.tile([P, 2 * PASSES * HALF_ROWS], U32, name="x_codes", align_bytes=64)
        x_scales = keep.tile([P, 2 * PASSES * HALF_ROWS], U8, name="x_scales", align_bytes=64)
        w_codes = keep.tile([P, N_TILES * TILE_WORDS], U32, name="w_codes", align_bytes=64)
        w_scales = keep.tile([P, N_TILES * TILE_WORDS], U8, name="w_scales", align_bytes=64)

        def channels_to_partitions(pairs):
            bank = t_banks.tile([P, CHUNKS, P], F32, tag="t", name="kt_bank")
            for c in range(CHUNKS):
                nc.tensor.transpose(bank[:, c, :], pairs[:, c * P : (c + 1) * P], ident[:])
            return bank[:].rearrange("p (g u) r -> p g r u", u=2)

        def quantise_x(half):
            grouped = stage.tile(
                [P, PACK * PASSES * HALF_ROWS], BF16, name="x_grouped", align_bytes=64
            )
            grouped_pairs = grouped[:].bitcast(F32).rearrange(
                "p (g j r u) -> p g j r u", g=PASSES, j=HALF_TILES, r=P, u=2
            )
            tiles_a_load = ROW_TILES // X_LOADS
            for j in range(HALF_TILES):
                row_tile = half * HALF_TILES + j
                pairs = x_raw[row_tile // tiles_a_load][:].bitcast(F32)
                first = (row_tile % tiles_a_load) * PAIRS
                side_by_side = channels_to_partitions(pairs[:, first : first + PAIRS])
                if j % 2 == 0:
                    nc.vector.tensor_copy(out=grouped_pairs[:, :, j], in_=side_by_side)
                else:
                    nc.scalar.copy(out=grouped_pairs[:, :, j], in_=side_by_side)
            for g in range(PASSES):
                cols = slice((half * PASSES + g) * HALF_ROWS, (half * PASSES + g + 1) * HALF_ROWS)
                nc.vector.quantize_mx(
                    out=x_codes[:, cols].bitcast(FP8X4),
                    scales=x_scales[:, cols],
                    in_=grouped[:, PACK * g * HALF_ROWS : PACK * (g + 1) * HALF_ROWS],
                )

        w_grouped = {}

        def regroup_w(i):
            grouped = w_stage.tile([P, PACK * TILE_WORDS], BF16, name="w_grouped", align_bytes=64)
            pairs = w_raw[i // HEAD_TILES][:].bitcast(F32)
            first = (i % HEAD_TILES) * PAIRS
            side_by_side = channels_to_partitions(pairs[:, first : first + PAIRS])
            nc.scalar.copy(
                out=grouped[:].bitcast(F32).rearrange("p (g m u) -> p g m u", g=PASSES, m=P, u=2),
                in_=side_by_side,
            )
            w_grouped[i] = grouped

        def quantise_w(i):
            cols = slice(i * TILE_WORDS, (i + 1) * TILE_WORDS)
            nc.vector.quantize_mx(
                out=w_codes[:, cols].bitcast(FP8X4), scales=w_scales[:, cols], in_=w_grouped[i][:]
            )

        y_of = {}
        y_copy_of = {}
        stats_of = {}
        mean_var_of = {}
        rstd_of = {}
        scales_of = {}
        shift_of = {}
        z_of = {}

        def project(i, half):
            if half == 0:
                stats_of[i] = small.tile([P, 2, BN_STATS_DIM], F32, name="stats")
                y_of[i] = []
            bank = y_banks.tile([P, HALF_ROWS], F32, tag="y", name="y_bank")
            for g in range(PASSES):
                w_cols = slice((i * PASSES + g) * P, (i * PASSES + g + 1) * P)
                x_cols = slice((half * PASSES + g) * HALF_ROWS, (half * PASSES + g + 1) * HALF_ROWS)
                nc.tensor.matmul_mx(
                    out=bank[:],
                    lhsT=w_codes[:, w_cols].bitcast(FP8X4),
                    lhsT_scale=w_scales[:, w_cols],
                    rhs=x_codes[:, x_cols].bitcast(FP8X4),
                    rhs_scale=x_scales[:, x_cols],
                    start=(g == 0),
                    stop=(g == PASSES - 1),
                )
            if i == 0 and half == 0:
                for n in range(W_LEAD, W_LEAD + 3):
                    regroup_w(n)
            nc.vector.bn_stats(out=stats_of[i][:, half, :], in_=bank[:])
            y_of[i].append(bank)
            if half == 0 and i < N_TILES - 1:
                y_copy = copied.tile([P, HALF_ROWS], F32, name="y_copy")
                nc.scalar.copy(out=y_copy[:], in_=bank[:])
                y_copy_of[i] = y_copy

        def aggregate(i):
            mean_var = small.tile([P, 2], F32, name="mean_var")
            nc.vector.bn_aggr(out=mean_var[:], in_=stats_of[i][:].rearrange("p a s -> p (a s)"))
            mean_var_of[i] = mean_var

        def reciprocal_root(i):
            rstd = small.tile([P, 1], F32, name="rstd")
            nc.scalar.activation(
                out=rstd[:], in_=mean_var_of[i][:, 1:2], func=ACT.Abs_reciprocal_sqrt, bias=EPS
            )
            rstd_of[i] = rstd

        def compute_scales(i):
            both = small.tile([P, 2], F32, name="scales")
            if i < N_TILES - 1:
                nc.gpsimd.tensor_scalar_mul(
                    out=both[:], in0=gain_pm[:, i, :], scalar1=rstd_of[i][:, 0:1]
                )
            else:
                nc.scalar.activation(
                    out=both[:], in_=gain_pm[:, i, :], func=ACT.Copy, scale=rstd_of[i][:, 0:1]
                )
            scales_of[i] = both

        def compute_shift(i):
            shift_i = small.tile([P, 1], F32, name="shift")
            mean = mean_var_of[i][:, 0:1]
            if i < N_TILES - 1:
                nc.gpsimd.tensor_scalar(
                    out=shift_i[:], in0=mean, scalar1=scales_of[i][:, 1:2],
                    scalar2=shift_in[:, i : i + 1], op0=ALU.mult, op1=ALU.add,
                )
            else:
                nc.scalar.activation(
                    out=shift_i[:], in_=mean, func=ACT.Identity,
                    scale=scales_of[i][:, 1:2], bias=shift_in[:, i : i + 1],
                )
            shift_of[i] = shift_i

        def normalise(i):
            z_first = normed.tile([P, HALF_ROWS], F32, name="z_first")
            z_second = normed.tile([P, HALF_ROWS], F32, name="z_second")
            nc.vector.tensor_scalar(
                out=z_second[:], in0=y_of[i][1][:], scalar1=scales_of[i][:, 0:1],
                scalar2=shift_of[i][:, 0:1], op0=ALU.mult, op1=ALU.add,
            )
            if i < N_TILES - 1:
                nc.gpsimd.tensor_scalar(
                    out=z_first[:], in0=y_copy_of[i][:], scalar1=scales_of[i][:, 0:1],
                    scalar2=shift_of[i][:, 0:1], op0=ALU.mult, op1=ALU.add,
                )
            else:
                nc.scalar.activation(
                    out=z_first[:], in_=y_of[i][0][:], func=ACT.Identity,
                    scale=scales_of[i][:, 0:1], bias=shift_of[i][:, 0:1],
                )
            z_of[i] = (z_first, z_second)

        def rows_to_partitions_and_store(i, vector_is_free, between=None):
            h = i // HEAD_TILES
            is_qk = i % HEAD_TILES == 0
            rows = result.tile([P, ROW_TILES * P], F32, name="rows")
            for half in (1, 0):
                bank = t_banks.tile([P, HALF_TILES, P], F32, tag="t", name="rows_bank")
                for j in range(HALF_TILES):
                    nc.tensor.transpose(bank[:, j, :], z_of[i][half][:, j * P : (j + 1) * P], ident[:])
                js = slice(half * HALF_TILES, (half + 1) * HALF_TILES)
                if is_qk:
                    dest = rows[:].rearrange("p (s j f) -> p s j f", s=2, j=ROW_TILES)[:, :, js, :]
                    source = bank[:].rearrange("p j (s f) -> p s j f", s=2)
                else:
                    dest = rows[:].rearrange("p (j f) -> p j f", j=ROW_TILES)[:, js, :]
                    source = bank[:]
                if vector_is_free and half == 0:
                    nc.vector.tensor_copy(out=dest, in_=source)
                else:
                    nc.scalar.copy(out=dest, in_=source)
                if half == 1 and between:
                    between()
                if not is_qk:
                    cols = slice(half * HALF_ROWS, (half + 1) * HALF_ROWS)
                    nc.sync.dma_start(out=v_rows[h][:, :, cols], in_=rows[:, cols])
            if is_qk:
                nc.sync.dma_start(out=q_rows[h], in_=rows[:, 0 : ROW_TILES * KD])
                nc.sync.dma_start(out=k_rows[h], in_=rows[:, ROW_TILES * KD :])

        gb_rows_f32 = keep.tile([P, P], F32, name="gb_rows_f32")
        gain_pm = keep.tile([P, N_TILES, 2], F32, name="gain_pm")
        shift_in = keep.tile([P, N_TILES], F32, name="shift_in")

        def turn_gain_and_shift():
            gb_bank = t_banks.tile([P, CHUNKS, P], F32, tag="t", name="gb_bank")
            nc.tensor.transpose(gb_bank[:, 0, :], gb_rows_f32[:], ident[:])
            gains = gb_bank[:, 0, 0:N_TILES]
            nc.vector.tensor_copy(out=gain_pm[:, :, 0], in_=gains)
            nc.vector.tensor_scalar_mul(out=gain_pm[:, :, 1], in0=gains, scalar1=-1.0)
            nc.vector.tensor_copy(
                out=shift_in[:], in_=gb_bank[:, 0, SHIFT_ROW : SHIFT_ROW + N_TILES]
            )

        quantise_x(0)
        nc.vector.tensor_copy(out=gb_rows_f32[:], in_=gb_rows[:])
        regroup_w(0)
        regroup_w(1)
        quantise_w(0)
        quantise_x(1)
        quantise_w(1)
        regroup_w(2)

        turned = W_LEAD + 3
        counts = [1, 2]
        for i in range(N_TILES + 2):
            enters = i < N_TILES
            if enters:
                project(i, 0)
            if 0 <= i - 1 < N_TILES - 1:
                compute_shift(i - 1)
            if enters:
                project(i, 1)
            if i == N_TILES - 1:
                aggregate(i)
            if 0 <= i - 1 < N_TILES - 1:
                normalise(i - 1)
            if i == 0:
                turn_gain_and_shift()
            if i < N_TILES - 1:
                aggregate(i)
            if i + W_LEAD - 1 < N_TILES:
                quantise_w(i + W_LEAD - 1)
            for n in range(counts[i] if i < len(counts) else 1):
                if turned < N_TILES:
                    regroup_w(turned)
                    turned += 1
            if i < 2:
                reciprocal_root(i)
                compute_scales(i)
            if i >= 2:
                if i == N_TILES - 1:
                    between = lambda: (reciprocal_root(i), compute_scales(i), compute_shift(i))
                elif enters:
                    between = lambda: (reciprocal_root(i), compute_scales(i))
                elif i == N_TILES:
                    between = lambda: normalise(i - 1)
                else:
                    between = None
                rows_to_partitions_and_store(i - 2, i >= N_TILES - 1, between)
